import numpy as np
import ml_dtypes


def mxq(x, axis, fmt="e4m3"):
    dtype, down = {"e4m3": (ml_dtypes.float8_e4m3fn, 7), "e5m2": (ml_dtypes.float8_e5m2, 14)}[fmt]
    v = np.moveaxis(np.asarray(x, np.float32).astype(ml_dtypes.bfloat16).astype(np.float64), axis, -1)
    blocks = v.reshape(v.shape[:-1] + (-1, 32))
    amax = np.abs(blocks).max(-1, keepdims=True)
    byte = np.maximum(np.where(amax > 0, np.frexp(amax)[1] - 1 + 127, 0) - down, 1)
    scale = np.exp2(byte - 127.0)
    codes = (blocks / scale).astype(np.float32).astype(dtype).astype(np.float64)
    return np.moveaxis((codes * scale).reshape(v.shape), -1, axis)


WIDE = False


def mx_kscale(k):
    if not WIDE:
        return np.ones(k)
    levels = np.array([10, -10, 5, -5, 0])
    a = np.random.permutation(np.resize(levels, k // 512 * 4)).reshape(k // 512, 4)
    idx = np.arange(k)
    return np.exp2(a[idx // 512, idx % 128 // 32])


BF16 = ml_dtypes.bfloat16


def bf(x):
    return np.asarray(x, np.float32).astype(BF16)


def f64(x):
    return np.asarray(x).astype(np.float64)


B, MI, MO, NL = 128, 1536, 1536, 4
IR_DIMS = tuple(2 * l + 1 for l in range(NL))
FLAT_IN = MI * sum(IR_DIMS)


def setup_inputs():
    s = mx_kscale(MI)
    sx = np.concatenate([np.repeat(s, d) for d in IR_DIMS])
    inp = {"x": bf(np.random.standard_normal((B, FLAT_IN)) * sx)}
    for l in range(NL):
        inp["W%d" % l] = bf(np.random.standard_normal((MO, MI)) / np.sqrt(MI) / s[None, :])
    inp["bias"] = bf(np.random.standard_normal(MO))
    return inp


def reference(x, W0, W1, W2, W3, bias):
    x = f64(x)
    outs = []
    start = 0
    for d, W in zip(IR_DIMS, (W0, W1, W2, W3)):
        seg = x[:, start:start + MI * d].reshape(B, MI, d)
        rows = seg.transpose(0, 2, 1).reshape(B * d, MI)
        y = mxq(rows, 1, "e4m3") @ mxq(f64(W).T, 0, "e4m3")
        outs.append(y.reshape(B, d, MO).transpose(0, 2, 1).reshape(B, MO * d))
        start += MI * d
    outs[0] = outs[0] + f64(bias)
    return np.concatenate(outs, axis=1)

@@ -1,0 +1,199 @@
+from contextlib import ExitStack
+
+import concourse.mybir as mybir
+from concourse.masks import make_identity
+
+F32 = mybir.dt.float32
+BF16 = mybir.dt.bfloat16
+U32 = mybir.dt.uint32
+U8 = mybir.dt.uint8
+FP8X4 = mybir.dt.float8_e4m3fn_x4
+
+P = 128
+CHANNELS = 1536
+IRREP_DIMS = (1, 3, 5, 7)
+SEGMENT_START = (0, 1536, 6144, 13824)
+K_PASS = 512
+THIRDS = CHANNELS // K_PASS
+HALVES = 2
+PASS_WORDS = K_PASS // 2
+CHUNK = 512
+ROWS = CHUNK // P
+LINE = 4
+
+SEGMENT_ORDER = (1, 2, 3, 0)
+
+X_LOAD_LEAD = 5
+X_SPLIT_LEAD = 4
+X_PACK_LEAD = 3
+W_LOAD_LEAD = 3
+W_PACK_LEAD = 1
+
+FLOPS = 2 * P * sum(IRREP_DIMS) * CHANNELS * CHANNELS
+
+
+def channels_to_partitions(nc, banks, identity, rows, grouped, drain):
+    bank = banks.tile([P, 2, HALVES, P], F32)
+    for s, words in enumerate(rows):
+        for u in range(HALVES):
+            nc.tensor.transpose(bank[:, s, u, :], words[:, u * P : (u + 1) * P], identity)
+    drain(out=grouped, in_=bank[:, : len(rows)].rearrange("p s u r -> p s r u"))
+
+
+def tile_so3_linear_pa_kernel(tc, x, W0, W1, W2, W3, bias, out):
+    nc = tc.nc
+    weights = (W0, W1, W2, W3)
+    steps = [(l, third) for l in SEGMENT_ORDER for third in range(THIRDS)]
+
+    with ExitStack() as ctx:
+        keep = ctx.enter_context(tc.tile_pool(name="keep", bufs=1))
+        stream = ctx.enter_context(tc.tile_pool(name="stream", bufs=2))
+        banks = ctx.enter_context(tc.psum_pool(name="banks", bufs=4))
+        sums = ctx.enter_context(tc.psum_pool(name="sums", bufs=4))
+        ctx.enter_context(tc.manual_schedule())
+
+        identity = keep.tile([P, P], F32)
+        make_identity(nc, identity[:])
+        bias_rows = keep.tile([P, CHANNELS], BF16)
+        x_codes = {}
+        x_scales = {}
+        for l, d in enumerate(IRREP_DIMS):
+            codes = keep.tile([P, THIRDS, d * P], U32, name="x_codes%d" % l, align_bytes=64)
+            scales = keep.tile([P, THIRDS, d * P], U8, name="x_scales%d" % l, align_bytes=64)
+            x_codes[l] = codes
+            x_scales[l] = scales
+        x_raw = {}
+        x_split = {}
+        w_raw = {}
+        w_packed = {}
+
+        def load_x(q):
+            l, g = steps[q]
+            d = IRREP_DIMS[l]
+            first = SEGMENT_START[l] + g * K_PASS * d
+            raw = stream.tile([P, K_PASS * d], BF16, name="x_raw", bufs=3)
+            nc.sync.dma_start(out=raw[:], in_=x[:, first : first + K_PASS * d])
+            x_raw[q] = raw
+
+        def split_x(q):
+            d = IRREP_DIMS[steps[q][0]]
+            split = stream.tile([P, d * K_PASS], BF16, name="x_split")
+            nc.vector.tensor_copy(
+                out=split[:].rearrange("p (i m) -> p i m", i=d),
+                in_=x_raw[q][:].rearrange("p (m i) -> p i m", i=d),
+            )
+            x_split[q] = split
+
+        def pack_x(q):
+            l, g = steps[q]
+            d = IRREP_DIMS[l]
+            words = x_split[q][:].bitcast(F32)
+            grouped = stream.tile([P, d * K_PASS], BF16, name="x_grouped", align_bytes=64)
+            grouped_words = grouped[:].bitcast(F32)
+            pairs = [(i, min(2, d - i)) for i in range(0, d, 2)]
+            for i, n in pairs:
+                channels_to_partitions(
+                    nc,
+                    banks,
+                    identity[:],
+                    [words[:, (i + s) * PASS_WORDS : (i + s + 1) * PASS_WORDS] for s in range(n)],
+                    grouped_words[:, i * PASS_WORDS : (i + n) * PASS_WORDS].rearrange(
+                        "p (s r u) -> p s r u", s=n, u=HALVES
+                    ),
+                    nc.vector.tensor_copy,
+                )
+            for i, n in pairs:
+                nc.vector.quantize_mx(
+                    out=x_codes[l][:, g, i * P : (i + n) * P].bitcast(FP8X4),
+                    scales=x_scales[l][:, g, i * P : (i + n) * P],
+                    in_=grouped[:, i * K_PASS : (i + n) * K_PASS],
+                )
+
+        def load_w(q):
+            l, c = steps[q]
+            raw = stream.tile([P, ROWS * CHANNELS], BF16, name="w_raw", bufs=3)
+            nc.sync.dma_start(
+                out=raw[:],
+                in_=weights[l][c * CHUNK : (c + 1) * CHUNK, :].rearrange("(j r) m -> j (r m)", r=ROWS),
+            )
+            w_raw[q] = raw
+
+        def pack_w(q):
+            words = w_raw[q][:].bitcast(F32)
+            row_words = CHANNELS // 2
+            grouped = stream.tile([P, THIRDS * CHUNK * 4], BF16, name="w_grouped", align_bytes=64)
+            grouped_words = grouped[:].bitcast(F32)
+            codes = stream.tile([P, THIRDS, CHUNK], U32, name="w_codes", align_bytes=64)
+            scales = stream.tile([P, THIRDS, CHUNK], U8, name="w_scales", align_bytes=64)
+            for g in range(THIRDS):
+                for r in range(0, ROWS, 2):
+                    first = (g * CHUNK + r * P) * HALVES
+                    channels_to_partitions(
+                        nc,
+                        banks,
+                        identity[:],
+                        [
+                            words[:, (r + s) * row_words + g * PASS_WORDS : (r + s) * row_words + (g + 1) * PASS_WORDS]
+                            for s in range(2)
+                        ],
+                        grouped_words[:, first : first + 2 * P * HALVES].rearrange(
+                            "p (s r u) -> p s r u", s=2, u=HALVES
+                        ),
+                        nc.scalar.copy,
+                    )
+                nc.vector.quantize_mx(
+                    out=codes[:, g, :].bitcast(FP8X4),
+                    scales=scales[:, g, :],
+                    in_=grouped[:, g * CHUNK * 4 : (g + 1) * CHUNK * 4],
+                )
+            w_packed[q] = (codes, scales)
+
+        def multiply(q):
+            l, c = steps[q]
+            d = IRREP_DIMS[l]
+            codes, scales = w_packed[q]
+            result = stream.tile([P, CHUNK * d], F32, name="result", bufs=3)
+            lines = result[:].rearrange("p (j k s) -> p j k s", k=d, s=LINE)
+            for k in range(d):
+                acc = sums.tile([P, LINE, P], F32)
+                for s in range(LINE):
+                    r, i = divmod(LINE * k + s, d)
+                    for g in range(THIRDS):
+                        nc.tensor.matmul_mx(
+                            out=acc[:, s, :],
+                            lhsT=x_codes[l][:, g, i * P : (i + 1) * P].bitcast(FP8X4),
+                            lhsT_scale=x_scales[l][:, g, i * P : (i + 1) * P],
+                            rhs=codes[:, g, r * P : (r + 1) * P].bitcast(FP8X4),
+                            rhs_scale=scales[:, g, r * P : (r + 1) * P],
+                            start=(g == 0),
+                            stop=(g == THIRDS - 1),
+                        )
+                by_line = acc[:].rearrange("p s j -> p j s")
+                if l == 0:
+                    nc.vector.tensor_tensor(
+                        out=lines[:, :, k, :],
+                        in0=by_line,
+                        in1=bias_rows[:, c * CHUNK : (c + 1) * CHUNK].rearrange("p (j s) -> p j s", s=LINE),
+                        op=mybir.AluOpType.add,
+                    )
+                else:
+                    nc.scalar.copy(out=lines[:, :, k, :], in_=by_line)
+            first = SEGMENT_START[l] + c * CHUNK * d
+            nc.scalar.dma_start(out=out[:, first : first + CHUNK * d], in_=result[:])
+
+        last = len(steps)
+        for now in range(-X_LOAD_LEAD, last):
+            if now + X_LOAD_LEAD < last:
+                load_x(now + X_LOAD_LEAD)
+            if now + X_LOAD_LEAD == last:
+                nc.sync.dma_start(out=bias_rows[:], in_=bias.partition_broadcast(P))
+            if 0 <= now + W_LOAD_LEAD < last:
+                load_w(now + W_LOAD_LEAD)
+            if 0 <= now + X_PACK_LEAD < last:
+                pack_x(now + X_PACK_LEAD)
+            if 0 <= now + W_PACK_LEAD < last:
+                pack_w(now + W_PACK_LEAD)
+            if 0 <= now + X_SPLIT_LEAD < last:
+                split_x(now + X_SPLIT_LEAD)
+            if 0 <= now:
+                multiply(now)

@@ -33,7 +33,7 @@ FLOPS = 2 * P * sum(IRREP_DIMS) * CHANNELS * CHANNELS
 
 
 def channels_to_partitions(nc, banks, identity, rows, grouped, drain):
-    bank = banks.tile([P, 2, HALVES, P], F32)
+    bank = banks.tile([P, 2, HALVES, P], F32, tag="bank")
     for s, words in enumerate(rows):
         for u in range(HALVES):
             nc.tensor.transpose(bank[:, s, u, :], words[:, u * P : (u + 1) * P], identity)
@@ -48,8 +48,7 @@ def tile_so3_linear_pa_kernel(tc, x, W0, W1, W2, W3, bias, out):
     with ExitStack() as ctx:
         keep = ctx.enter_context(tc.tile_pool(name="keep", bufs=1))
         stream = ctx.enter_context(tc.tile_pool(name="stream", bufs=2))
-        banks = ctx.enter_context(tc.psum_pool(name="banks", bufs=4))
-        sums = ctx.enter_context(tc.psum_pool(name="sums", bufs=4))
+        banks = ctx.enter_context(tc.psum_pool(name="banks", bufs=8))
         ctx.enter_context(tc.manual_schedule())
 
         identity = keep.tile([P, P], F32)
@@ -155,7 +154,7 @@ def tile_so3_linear_pa_kernel(tc, x, W0, W1, W2, W3, bias, out):
             result = stream.tile([P, CHUNK * d], F32, name="result", bufs=3)
             lines = result[:].rearrange("p (j k s) -> p j k s", k=d, s=LINE)
             for k in range(d):
-                acc = sums.tile([P, LINE, P], F32)
+                acc = banks.tile([P, LINE, P], F32, tag="bank")
                 for s in range(LINE):
                     r, i = divmod(LINE * k + s, d)
                     for g in range(THIRDS):

@@ -23,11 +23,11 @@ LINE = 4
 
 SEGMENT_ORDER = (1, 2, 3, 0)
 
-X_LOAD_LEAD = 5
-X_SPLIT_LEAD = 4
+X_LOAD_LEAD = 6
+X_SPLIT_LEAD = 5
 X_PACK_LEAD = 3
-W_LOAD_LEAD = 3
-W_PACK_LEAD = 1
+W_LOAD_LEAD = 4
+W_PACK_LEAD = 2
 
 FLOPS = 2 * P * sum(IRREP_DIMS) * CHANNELS * CHANNELS
 
@@ -70,13 +70,13 @@ def tile_so3_linear_pa_kernel(tc, x, W0, W1, W2, W3, bias, out):
             l, g = steps[q]
             d = IRREP_DIMS[l]
             first = SEGMENT_START[l] + g * K_PASS * d
-            raw = stream.tile([P, K_PASS * d], BF16, name="x_raw", bufs=3)
+            raw = stream.tile([P, K_PASS * d], BF16, name="x_raw", bufs=4)
             nc.sync.dma_start(out=raw[:], in_=x[:, first : first + K_PASS * d])
             x_raw[q] = raw
 
         def split_x(q):
             d = IRREP_DIMS[steps[q][0]]
-            split = stream.tile([P, d * K_PASS], BF16, name="x_split")
+            split = stream.tile([P, d * K_PASS], BF16, name="x_split", bufs=3)
             nc.vector.tensor_copy(
                 out=split[:].rearrange("p (i m) -> p i m", i=d),
                 in_=x_raw[q][:].rearrange("p (m i) -> p i m", i=d),
@@ -122,8 +122,8 @@ def tile_so3_linear_pa_kernel(tc, x, W0, W1, W2, W3, bias, out):
             row_words = CHANNELS // 2
             grouped = stream.tile([P, THIRDS * CHUNK * 4], BF16, name="w_grouped", align_bytes=64)
             grouped_words = grouped[:].bitcast(F32)
-            codes = stream.tile([P, THIRDS, CHUNK], U32, name="w_codes", align_bytes=64)
-            scales = stream.tile([P, THIRDS, CHUNK], U8, name="w_scales", align_bytes=64)
+            codes = stream.tile([P, THIRDS, CHUNK], U32, name="w_codes", bufs=3, align_bytes=64)
+            scales = stream.tile([P, THIRDS, CHUNK], U8, name="w_scales", bufs=3, align_bytes=64)
             for g in range(THIRDS):
                 for r in range(0, ROWS, 2):
                     first = (g * CHUNK + r * P) * HALVES
@@ -182,16 +182,16 @@ def tile_so3_linear_pa_kernel(tc, x, W0, W1, W2, W3, bias, out):
 
         last = len(steps)
         for now in range(-X_LOAD_LEAD, last):
+            if 0 <= now + W_LOAD_LEAD < last:
+                load_w(now + W_LOAD_LEAD)
             if now + X_LOAD_LEAD < last:
                 load_x(now + X_LOAD_LEAD)
             if now + X_LOAD_LEAD == last:
                 nc.sync.dma_start(out=bias_rows[:], in_=bias.partition_broadcast(P))
-            if 0 <= now + W_LOAD_LEAD < last:
-                load_w(now + W_LOAD_LEAD)
-            if 0 <= now + X_PACK_LEAD < last:
-                pack_x(now + X_PACK_LEAD)
             if 0 <= now + W_PACK_LEAD < last:
                 pack_w(now + W_PACK_LEAD)
+            if 0 <= now + X_PACK_LEAD < last:
+                pack_x(now + X_PACK_LEAD)
             if 0 <= now + X_SPLIT_LEAD < last:
                 split_x(now + X_SPLIT_LEAD)
             if 0 <= now:

@@ -77,10 +77,16 @@ def tile_so3_linear_pa_kernel(tc, x, W0, W1, W2, W3, bias, out):
         def split_x(q):
             d = IRREP_DIMS[steps[q][0]]
             split = stream.tile([P, d * K_PASS], BF16, name="x_split", bufs=3)
-            nc.vector.tensor_copy(
-                out=split[:].rearrange("p (i m) -> p i m", i=d),
-                in_=x_raw[q][:].rearrange("p (m i) -> p i m", i=d),
-            )
+            by_component = x_raw[q][:].rearrange("p (m i) -> p i m", i=d)
+            for i in range(d):
+                nc.gpsimd.tensor_scalar(
+                    out=split[:, i * K_PASS : (i + 1) * K_PASS],
+                    in0=by_component[:, i, :],
+                    scalar1=1.0,
+                    scalar2=0.0,
+                    op0=mybir.AluOpType.mult,
+                    op1=mybir.AluOpType.add,
+                )
             x_split[q] = split
 
         def pack_x(q):

@@ -19,7 +19,6 @@ HALVES = 2
 PASS_WORDS = K_PASS // 2
 CHUNK = 512
 ROWS = CHUNK // P
-LINE = 4
 
 SEGMENT_ORDER = (1, 2, 3, 0)
 
@@ -70,7 +69,7 @@ def tile_so3_linear_pa_kernel(tc, x, W0, W1, W2, W3, bias, out):
             l, g = steps[q]
             d = IRREP_DIMS[l]
             first = SEGMENT_START[l] + g * K_PASS * d
-            raw = stream.tile([P, K_PASS * d], BF16, name="x_raw", bufs=4)
+            raw = stream.tile([P, K_PASS * d], BF16, name="x_raw", bufs=3)
             nc.sync.dma_start(out=raw[:], in_=x[:, first : first + K_PASS * d])
             x_raw[q] = raw
 
@@ -157,34 +156,41 @@ def tile_so3_linear_pa_kernel(tc, x, W0, W1, W2, W3, bias, out):
             l, c = steps[q]
             d = IRREP_DIMS[l]
             codes, scales = w_packed[q]
-            result = stream.tile([P, CHUNK * d], F32, name="result", bufs=3)
-            lines = result[:].rearrange("p (j k s) -> p j k s", k=d, s=LINE)
-            for k in range(d):
-                acc = banks.tile([P, LINE, P], F32, tag="bank")
-                for s in range(LINE):
-                    r, i = divmod(LINE * k + s, d)
-                    for g in range(THIRDS):
-                        nc.tensor.matmul_mx(
-                            out=acc[:, s, :],
-                            lhsT=x_codes[l][:, g, i * P : (i + 1) * P].bitcast(FP8X4),
-                            lhsT_scale=x_scales[l][:, g, i * P : (i + 1) * P],
-                            rhs=codes[:, g, r * P : (r + 1) * P].bitcast(FP8X4),
-                            rhs_scale=scales[:, g, r * P : (r + 1) * P],
-                            start=(g == 0),
-                            stop=(g == THIRDS - 1),
-                        )
-                by_line = acc[:].rearrange("p s j -> p j s")
+            result = stream.tile([P, CHUNK * d], F32, name="result")
+            if l > 0:
+                planes = stream.tile([P, d * CHUNK], F32, name="planes")
+            for i in range(d):
+                acc = banks.tile([P, CHUNK], F32, tag="bank")
+                for g in range(THIRDS):
+                    nc.tensor.matmul_mx(
+                        out=acc[:],
+                        lhsT=x_codes[l][:, g, i * P : (i + 1) * P].bitcast(FP8X4),
+                        lhsT_scale=x_scales[l][:, g, i * P : (i + 1) * P],
+                        rhs=codes[:, g, :].bitcast(FP8X4),
+                        rhs_scale=scales[:, g, :],
+                        start=(g == 0),
+                        stop=(g == THIRDS - 1),
+                    )
+                in_order = acc[:].rearrange("p (r j) -> p j r", r=ROWS)
                 if l == 0:
                     nc.vector.tensor_tensor(
-                        out=lines[:, :, k, :],
-                        in0=by_line,
-                        in1=bias_rows[:, c * CHUNK : (c + 1) * CHUNK].rearrange("p (j s) -> p j s", s=LINE),
+                        out=result[:].rearrange("p (j r) -> p j r", r=ROWS),
+                        in0=in_order,
+                        in1=bias_rows[:, c * CHUNK : (c + 1) * CHUNK].rearrange("p (j r) -> p j r", r=ROWS),
                         op=mybir.AluOpType.add,
                     )
                 else:
-                    nc.scalar.copy(out=lines[:, :, k, :], in_=by_line)
+                    nc.scalar.copy(
+                        out=planes[:, i * CHUNK : (i + 1) * CHUNK].rearrange("p (j r) -> p j r", r=ROWS),
+                        in_=in_order,
+                    )
+            if l > 0:
+                nc.vector.tensor_copy(
+                    out=result[:].rearrange("p (n i) -> p n i", i=d),
+                    in_=planes[:].rearrange("p (i n) -> p n i", i=d),
+                )
             first = SEGMENT_START[l] + c * CHUNK * d
-            nc.scalar.dma_start(out=out[:, first : first + CHUNK * d], in_=result[:])
+            nc.sync.dma_start(out=out[:, first : first + CHUNK * d], in_=result[:])
 
         last = len(steps)
         for now in range(-X_LOAD_LEAD, last):

from contextlib import ExitStack

import concourse.mybir as mybir
from concourse.masks import make_identity

F32 = mybir.dt.float32
BF16 = mybir.dt.bfloat16
U32 = mybir.dt.uint32
U8 = mybir.dt.uint8
FP8X4 = mybir.dt.float8_e4m3fn_x4

P = 128
CHANNELS = 1536
IRREP_DIMS = (1, 3, 5, 7)
SEGMENT_START = (0, 1536, 6144, 13824)
K_PASS = 512
THIRDS = CHANNELS // K_PASS
HALVES = 2
PASS_WORDS = K_PASS // 2
CHUNK = 512
ROWS = CHUNK // P

SEGMENT_ORDER = (1, 2, 3, 0)

X_LOAD_LEAD = 6
X_SPLIT_LEAD = 5
X_PACK_LEAD = 3
W_LOAD_LEAD = 4
W_PACK_LEAD = 2

FLOPS = 2 * P * sum(IRREP_DIMS) * CHANNELS * CHANNELS


def channels_to_partitions(nc, banks, identity, rows, grouped, drain):
    bank = banks.tile([P, 2, HALVES, P], F32, tag="bank")
    for s, words in enumerate(rows):
        for u in range(HALVES):
            nc.tensor.transpose(bank[:, s, u, :], words[:, u * P : (u + 1) * P], identity)
    drain(out=grouped, in_=bank[:, : len(rows)].rearrange("p s u r -> p s r u"))


def tile_so3_linear_pa_kernel(tc, x, W0, W1, W2, W3, bias, out):
    nc = tc.nc
    weights = (W0, W1, W2, W3)
    steps = [(l, third) for l in SEGMENT_ORDER for third in range(THIRDS)]

    with ExitStack() as ctx:
        keep = ctx.enter_context(tc.tile_pool(name="keep", bufs=1))
        stream = ctx.enter_context(tc.tile_pool(name="stream", bufs=2))
        banks = ctx.enter_context(tc.psum_pool(name="banks", bufs=8))
        ctx.enter_context(tc.manual_schedule())

        identity = keep.tile([P, P], F32)
        make_identity(nc, identity[:])
        bias_rows = keep.tile([P, CHANNELS], BF16)
        x_codes = {}
        x_scales = {}
        for l, d in enumerate(IRREP_DIMS):
            codes = keep.tile([P, THIRDS, d * P], U32, name="x_codes%d" % l, align_bytes=64)
            scales = keep.tile([P, THIRDS, d * P], U8, name="x_scales%d" % l, align_bytes=64)
            x_codes[l] = codes
            x_scales[l] = scales
        x_raw = {}
        x_split = {}
        w_raw = {}
        w_packed = {}

        def load_x(q):
            l, g = steps[q]
            d = IRREP_DIMS[l]
            first = SEGMENT_START[l] + g * K_PASS * d
            raw = stream.tile([P, K_PASS * d], BF16, name="x_raw", bufs=3)
            nc.sync.dma_start(out=raw[:], in_=x[:, first : first + K_PASS * d])
            x_raw[q] = raw

        def split_x(q):
            d = IRREP_DIMS[steps[q][0]]
            split = stream.tile([P, d * K_PASS], BF16, name="x_split", bufs=3)
            by_component = x_raw[q][:].rearrange("p (m i) -> p i m", i=d)
            for i in range(d):
                nc.gpsimd.tensor_scalar(
                    out=split[:, i * K_PASS : (i + 1) * K_PASS],
                    in0=by_component[:, i, :],
                    scalar1=1.0,
                    scalar2=0.0,
                    op0=mybir.AluOpType.mult,
                    op1=mybir.AluOpType.add,
                )
            x_split[q] = split

        def pack_x(q):
            l, g = steps[q]
            d = IRREP_DIMS[l]
            words = x_split[q][:].bitcast(F32)
            grouped = stream.tile([P, d * K_PASS], BF16, name="x_grouped", align_bytes=64)
            grouped_words = grouped[:].bitcast(F32)
            pairs = [(i, min(2, d - i)) for i in range(0, d, 2)]
            for i, n in pairs:
                channels_to_partitions(
                    nc,
                    banks,
                    identity[:],
                    [words[:, (i + s) * PASS_WORDS : (i + s + 1) * PASS_WORDS] for s in range(n)],
                    grouped_words[:, i * PASS_WORDS : (i + n) * PASS_WORDS].rearrange(
                        "p (s r u) -> p s r u", s=n, u=HALVES
                    ),
                    nc.vector.tensor_copy,
                )
            for i, n in pairs:
                nc.vector.quantize_mx(
                    out=x_codes[l][:, g, i * P : (i + n) * P].bitcast(FP8X4),
                    scales=x_scales[l][:, g, i * P : (i + n) * P],
                    in_=grouped[:, i * K_PASS : (i + n) * K_PASS],
                )

        def load_w(q):
            l, c = steps[q]
            raw = stream.tile([P, ROWS * CHANNELS], BF16, name="w_raw", bufs=3)
            nc.sync.dma_start(
                out=raw[:],
                in_=weights[l][c * CHUNK : (c + 1) * CHUNK, :].rearrange("(j r) m -> j (r m)", r=ROWS),
            )
            w_raw[q] = raw

        def pack_w(q):
            words = w_raw[q][:].bitcast(F32)
            row_words = CHANNELS // 2
            grouped = stream.tile([P, THIRDS * CHUNK * 4], BF16, name="w_grouped", align_bytes=64)
            grouped_words = grouped[:].bitcast(F32)
            codes = stream.tile([P, THIRDS, CHUNK], U32, name="w_codes", bufs=3, align_bytes=64)
            scales = stream.tile([P, THIRDS, CHUNK], U8, name="w_scales", bufs=3, align_bytes=64)
            for g in range(THIRDS):
                for r in range(0, ROWS, 2):
                    first = (g * CHUNK + r * P) * HALVES
                    channels_to_partitions(
                        nc,
                        banks,
                        identity[:],
                        [
                            words[:, (r + s) * row_words + g * PASS_WORDS : (r + s) * row_words + (g + 1) * PASS_WORDS]
                            for s in range(2)
                        ],
                        grouped_words[:, first : first + 2 * P * HALVES].rearrange(
                            "p (s r u) -> p s r u", s=2, u=HALVES
                        ),
                        nc.scalar.copy,
                    )
                nc.vector.quantize_mx(
                    out=codes[:, g, :].bitcast(FP8X4),
                    scales=scales[:, g, :],
                    in_=grouped[:, g * CHUNK * 4 : (g + 1) * CHUNK * 4],
                )
            w_packed[q] = (codes, scales)

        def multiply(q):
            l, c = steps[q]
            d = IRREP_DIMS[l]
            codes, scales = w_packed[q]
            result = stream.tile([P, CHUNK * d], F32, name="result")
            if l > 0:
                planes = stream.tile([P, d * CHUNK], F32, name="planes")
            for i in range(d):
                acc = banks.tile([P, CHUNK], F32, tag="bank")
                for g in range(THIRDS):
                    nc.tensor.matmul_mx(
                        out=acc[:],
                        lhsT=x_codes[l][:, g, i * P : (i + 1) * P].bitcast(FP8X4),
                        lhsT_scale=x_scales[l][:, g, i * P : (i + 1) * P],
                        rhs=codes[:, g, :].bitcast(FP8X4),
                        rhs_scale=scales[:, g, :],
                        start=(g == 0),
                        stop=(g == THIRDS - 1),
                    )
                in_order = acc[:].rearrange("p (r j) -> p j r", r=ROWS)
                if l == 0:
                    nc.vector.tensor_tensor(
                        out=result[:].rearrange("p (j r) -> p j r", r=ROWS),
                        in0=in_order,
                        in1=bias_rows[:, c * CHUNK : (c + 1) * CHUNK].rearrange("p (j r) -> p j r", r=ROWS),
                        op=mybir.AluOpType.add,
                    )
                else:
                    nc.scalar.copy(
                        out=planes[:, i * CHUNK : (i + 1) * CHUNK].rearrange("p (j r) -> p j r", r=ROWS),
                        in_=in_order,
                    )
            if l > 0:
                nc.vector.tensor_copy(
                    out=result[:].rearrange("p (n i) -> p n i", i=d),
                    in_=planes[:].rearrange("p (i n) -> p n i", i=d),
                )
            first = SEGMENT_START[l] + c * CHUNK * d
            nc.sync.dma_start(out=out[:, first : first + CHUNK * d], in_=result[:])

        last = len(steps)
        for now in range(-X_LOAD_LEAD, last):
            if 0 <= now + W_LOAD_LEAD < last:
                load_w(now + W_LOAD_LEAD)
            if now + X_LOAD_LEAD < last:
                load_x(now + X_LOAD_LEAD)
            if now + X_LOAD_LEAD == last:
                nc.sync.dma_start(out=bias_rows[:], in_=bias.partition_broadcast(P))
            if 0 <= now + W_PACK_LEAD < last:
                pack_w(now + W_PACK_LEAD)
            if 0 <= now + X_PACK_LEAD < last:
                pack_x(now + X_PACK_LEAD)
            if 0 <= now + X_SPLIT_LEAD < last:
                split_x(now + X_SPLIT_LEAD)
            if 0 <= now:
                multiply(now)
